import numpy as np
import ml_dtypes


def mxq(x, axis, fmt="e4m3"):
    dtype, down = {"e4m3": (ml_dtypes.float8_e4m3fn, 7), "e5m2": (ml_dtypes.float8_e5m2, 14)}[fmt]
    v = np.moveaxis(np.asarray(x, np.float32).astype(ml_dtypes.bfloat16).astype(np.float64), axis, -1)
    blocks = v.reshape(v.shape[:-1] + (-1, 32))
    amax = np.abs(blocks).max(-1, keepdims=True)
    byte = np.maximum(np.where(amax > 0, np.frexp(amax)[1] - 1 + 127, 0) - down, 1)
    scale = np.exp2(byte - 127.0)
    codes = (blocks / scale).astype(np.float32).astype(dtype).astype(np.float64)
    return np.moveaxis((codes * scale).reshape(v.shape), -1, axis)


WIDE = False


def mx_kscale(k):
    if not WIDE:
        return np.ones(k)
    levels = np.array([10, -10, 5, -5, 0])
    if k % 512:
        return np.exp2(np.random.permutation(np.resize(levels, k // 32))).repeat(32)
    a = np.empty((k // 512, 16))
    for p in range(k // 512):
        a[p, :8] = np.random.permutation(np.resize(levels, 8))
        for g in range(8):
            far = levels[np.abs(levels - a[p, g]) >= 10]
            a[p, g + 8] = far[np.random.randint(len(far))]
    return np.exp2(a.ravel()).repeat(32)


BF16 = ml_dtypes.bfloat16


def bf(x):
    return np.asarray(x, np.float32).astype(BF16)


def f64(x):
    return np.asarray(x).astype(np.float64)


M, P, D = 16384, 512, 128


def setup_inputs():
    s = mx_kscale(P)
    return {"G": bf(np.exp(-np.abs(3.0 + np.random.standard_normal((M, P)))) * s[None, :]),
            "x_next": bf(np.random.standard_normal((P, D)) * 1.5 * (s.mean() / s)[:, None])}


def reference(G, x_next):
    g = f64(G)
    p = g / np.sum(g, axis=1, keepdims=True)
    return mxq(p, 1, "e4m3") @ mxq(f64(x_next), 0, "e4m3")

@@ -1,0 +1,244 @@
+from contextlib import ExitStack
+
+import concourse.mybir as mybir
+from concourse.masks import make_identity
+
+F32 = mybir.dt.float32
+BF16 = mybir.dt.bfloat16
+U32 = mybir.dt.uint32
+U8 = mybir.dt.uint8
+FP8X4 = mybir.dt.float8_e4m3fn_x4
+MULT = mybir.AluOpType.mult
+ADD = mybir.AluOpType.add
+
+P = 128
+M, K, D = 16384, 512, 128
+PACK = 4
+TILES = M // P
+GROUP = 4
+QUADS = TILES // GROUP
+FLOPS = 2 * M * K * D
+
+LAG = 4
+AHEAD = 8
+TAIL_C = 1
+TAIL_E = 1
+E_ON_V_EVERY = 0
+S_SUM_TILE = 1
+S_SUM_EVERY = 8
+S_SUM_AHEAD = 2
+COPY = mybir.ActivationFunctionType.Copy
+
+
+def tile_nntransformlearner_pb_t_kernel(tc, G, x_next, out):
+    nc = tc.nc
+    g_view = G.rearrange("(p c) k -> p c k", c=TILES)
+    out_view = out.rearrange("(p c) d -> p c d", c=TILES)
+    with ExitStack() as ctx:
+        const = ctx.enter_context(tc.tile_pool(name="const", bufs=1))
+        gpool = ctx.enter_context(tc.tile_pool(name="gpool", bufs=AHEAD + 2))
+        small = ctx.enter_context(tc.tile_pool(name="small", bufs=6))
+        ppool = ctx.enter_context(tc.tile_pool(name="ppool", bufs=3))
+        qpool = ctx.enter_context(tc.tile_pool(name="qpool", bufs=LAG + 2))
+        cpool = ctx.enter_context(tc.tile_pool(name="cpool", bufs=3))
+        opool = ctx.enter_context(tc.tile_pool(name="opool", bufs=4))
+        psum_t = ctx.enter_context(tc.psum_pool(name="psum_t", bufs=5))
+        psum_o = ctx.enter_context(tc.psum_pool(name="psum_o", bufs=3))
+        ctx.enter_context(tc.manual_schedule())
+
+        g_tiles = {}
+        sums_t = {}
+        recip_t = {}
+        p_tiles = {}
+        xt_t = {}
+        grouped_t = {}
+        codes_t = {}
+        scales_t = {}
+        acc_t = {}
+
+        def e_on_vector(q):
+            if q >= QUADS - TAIL_E:
+                return True
+            return E_ON_V_EVERY > 0 and q % E_ON_V_EVERY == E_ON_V_EVERY - 1
+
+        def c_on_vector(n):
+            return n >= TILES - GROUP * TAIL_C and n % 2 == 1
+
+        def sum_on_scalar(n):
+            q, j = divmod(n, GROUP)
+            if j != S_SUM_TILE or q == 0 or q >= QUADS:
+                return False
+            return q <= 2 or q % S_SUM_EVERY == S_SUM_EVERY - 1
+
+        def pieces(q):
+            if q == QUADS - 1:
+                return [(0, GROUP // 2), (GROUP // 2, GROUP)]
+            return [(0, GROUP)]
+
+        def load(q):
+            g_sb = gpool.tile([P, GROUP, K], BF16, name="g_sb")
+            g_tiles[q] = g_sb
+            if q == 0:
+                for j in range(GROUP):
+                    nc.sync.dma_start(out=g_sb[:, j, :], in_=g_view[:, j, :])
+            else:
+                nc.sync.dma_start(out=g_sb[:], in_=g_view[:, q * GROUP : (q + 1) * GROUP, :])
+
+        def new_quad(q):
+            sums_t[q] = small.tile([P, GROUP, 8], F32, name="sums")
+            recip_t[q] = small.tile([P, GROUP], F32, name="recip")
+
+        def row_sum_scalar(n):
+            q, j = divmod(n, GROUP)
+            nc.scalar.activation(
+                out=junk_s[:, q % 2, :],
+                in_=g_tiles[q][:, j, :],
+                func=COPY,
+                accum_out=sums_t[q][:, j, 0:1],
+            )
+
+        def row_sum(n):
+            q, j = divmod(n, GROUP)
+            if j == 0:
+                p_tiles[q] = ppool.tile([P, GROUP, K], BF16, name="p_sb")
+            if sum_on_scalar(n):
+                return
+            nc.vector.scalar_tensor_tensor(
+                out=junk[:, j, :],
+                in0=g_tiles[q][:, j, 0 : K // 2],
+                scalar=1.0,
+                in1=g_tiles[q][:, j, K // 2 : K],
+                op0=MULT,
+                op1=ADD,
+                accum_out=sums_t[q][:, j, 0:1],
+            )
+
+        def reciprocals(q, first, last):
+            nc.vector.reciprocal(recip_t[q][:, first:last], sums_t[q][:, first:last, 0])
+
+        def normalise(n):
+            q, j = divmod(n, GROUP)
+            nc.vector.tensor_scalar(
+                out=p_tiles[q][:, j, :],
+                in0=g_tiles[q][:, j, :],
+                scalar1=recip_t[q][:, j : j + 1],
+                scalar2=None,
+                op0=MULT,
+            )
+
+        def transpose(n):
+            q, j = divmod(n, GROUP)
+            xt = psum_t.tile([P, 2, P], F32, name="xt")
+            xt_t[n] = xt
+            words = p_tiles[q][:, j, :].bitcast(F32)
+            for u in range(2):
+                nc.tensor.transpose(xt[:, u, :], words[:, u : K // 2 : 2], ident[:])
+
+        def regroup(n, engine_copy):
+            q, j = divmod(n, GROUP)
+            engine_copy(
+                out=grouped_t[q][:, j, :, :].rearrange("p m t -> p (m t)").bitcast(F32).rearrange("p (m u) -> p m u", u=2),
+                in_=xt_t[n][:].rearrange("p u m -> p m u"),
+            )
+
+        def quantise(q, first, last):
+            if first == 0:
+                codes_t[q] = cpool.tile([P, GROUP * P], U32, name="codes", align_bytes=64)
+                scales_t[q] = cpool.tile([P, GROUP * P], U8, name="scales", align_bytes=64)
+            nc.vector.quantize_mx(
+                out=codes_t[q][:, first * P : last * P].bitcast(FP8X4),
+                scales=scales_t[q][:, first * P : last * P],
+                in_=grouped_t[q][:, first:last, :, :].rearrange("p j m t -> p (j m t)"),
+            )
+
+        def multiply(q, first, last):
+            acc_t[q, first] = psum_o.tile([P, GROUP, D], F32, name="acc")
+            for j in range(first, last):
+                nc.tensor.matmul_mx(
+                    out=acc_t[q, first][:, j, :],
+                    lhsT=codes_t[q][:, j * P : (j + 1) * P].bitcast(FP8X4),
+                    lhsT_scale=scales_t[q][:, j * P : (j + 1) * P],
+                    rhs=x_codes[:].bitcast(FP8X4),
+                    rhs_scale=x_scales[:],
+                    start=True,
+                    stop=True,
+                )
+
+        def store(q, first, last, engine_copy):
+            o_sb = opool.tile([P, GROUP, D], F32, name="o_sb")
+            engine_copy(out=o_sb[:, first:last, :], in_=acc_t[q, first][:, first:last, :])
+            nc.sync.dma_start(
+                out=out_view[:, q * GROUP + first : q * GROUP + last, :], in_=o_sb[:, first:last, :]
+            )
+
+        x_raw = const.tile([P, PACK, D], BF16)
+        for q in range(AHEAD):
+            load(q)
+            if q == 1:
+                nc.sync.dma_start(out=x_raw[:], in_=x_next.rearrange("(p t) d -> p t d", t=PACK))
+        ident = const.tile([P, P], F32)
+        make_identity(nc, ident[:])
+        junk = const.tile([P, GROUP, K // 2], F32)
+        junk_s = const.tile([P, 2, K], BF16)
+        x_grouped = const.tile([P, D, PACK], BF16, align_bytes=64)
+        x_codes = const.tile([P, D], U32, align_bytes=64)
+        x_scales = const.tile([P, D], U8, align_bytes=64)
+
+        for q in range(S_SUM_AHEAD):
+            new_quad(q)
+            for j in range(GROUP):
+                if sum_on_scalar(q * GROUP + j):
+                    row_sum_scalar(q * GROUP + j)
+        row_sum(0)
+        for s in range(QUADS + LAG + 2):
+            if s + AHEAD < QUADS:
+                load(s + AHEAD)
+            if s + S_SUM_AHEAD < QUADS:
+                new_quad(s + S_SUM_AHEAD)
+                for j in range(GROUP):
+                    if sum_on_scalar((s + S_SUM_AHEAD) * GROUP + j):
+                        row_sum_scalar((s + S_SUM_AHEAD) * GROUP + j)
+            if s == 0:
+                for j in range(GROUP):
+                    row_sum(j + 1)
+                    reciprocals(0, j, j + 1)
+                    normalise(j)
+            elif s < QUADS:
+                for j in range(1, GROUP):
+                    row_sum(s * GROUP + j)
+            if 0 <= s - LAG < QUADS:
+                for first, last in pieces(s - LAG):
+                    quantise(s - LAG, first, last)
+            if 0 <= s - 1 < QUADS:
+                for j in range(GROUP):
+                    if c_on_vector((s - 1) * GROUP + j):
+                        regroup((s - 1) * GROUP + j, nc.vector.tensor_copy)
+            if 0 <= s - LAG - 1 < QUADS and e_on_vector(s - LAG - 1):
+                first, last = pieces(s - LAG - 1)[-1]
+                store(s - LAG - 1, first, last, nc.vector.tensor_copy)
+            if 0 < s < QUADS:
+                reciprocals(s, 0, GROUP)
+                if s + 1 < QUADS:
+                    row_sum((s + 1) * GROUP)
+                for j in range(GROUP):
+                    normalise(s * GROUP + j)
+            if s == 2:
+                nc.vector.quantize_mx(
+                    out=x_codes[:].bitcast(FP8X4),
+                    scales=x_scales[:],
+                    in_=x_grouped[:].rearrange("p d t -> p (d t)"),
+                )
+            if 0 <= s - LAG < QUADS:
+                for first, last in pieces(s - LAG):
+                    multiply(s - LAG, first, last)
+                    if last < GROUP or not e_on_vector(s - LAG):
+                        store(s - LAG, first, last, nc.scalar.copy)
+            if s < QUADS:
+                grouped_t[s] = qpool.tile([P, GROUP, P, PACK], BF16, name="grouped", align_bytes=64)
+                for j in range(GROUP):
+                    transpose(s * GROUP + j)
+                for j in range(GROUP):
+                    if not c_on_vector(s * GROUP + j):
+                        regroup(s * GROUP + j, nc.scalar.copy)
+            if s == 0:
+                nc.scalar.copy(out=x_grouped[:], in_=x_raw[:].rearrange("p t d -> p d t"))

@@ -25,7 +25,6 @@ TAIL_C = 1
 TAIL_E = 1
 E_ON_V_EVERY = 0
 S_SUM_TILE = 1
-S_SUM_EVERY = 8
 S_SUM_AHEAD = 2
 COPY = mybir.ActivationFunctionType.Copy
 
@@ -66,9 +65,7 @@ def tile_nntransformlearner_pb_t_kernel(tc, G, x_next, out):
 
         def sum_on_scalar(n):
             q, j = divmod(n, GROUP)
-            if j != S_SUM_TILE or q == 0 or q >= QUADS:
-                return False
-            return q <= 2 or q % S_SUM_EVERY == S_SUM_EVERY - 1
+            return j == S_SUM_TILE and 0 < q < QUADS
 
         def pieces(q):
             if q == QUADS - 1:

@@ -25,6 +25,7 @@ TAIL_C = 1
 TAIL_E = 1
 E_ON_V_EVERY = 0
 S_SUM_TILE = 1
+G_NORM_TILE = 0
 S_SUM_AHEAD = 2
 COPY = mybir.ActivationFunctionType.Copy
 
@@ -67,6 +68,10 @@ def tile_nntransformlearner_pb_t_kernel(tc, G, x_next, out):
             q, j = divmod(n, GROUP)
             return j == S_SUM_TILE and 0 < q < QUADS
 
+        def norm_on_gpsimd(n):
+            q, j = divmod(n, GROUP)
+            return j == G_NORM_TILE and 0 < q < QUADS - 1
+
         def pieces(q):
             if q == QUADS - 1:
                 return [(0, GROUP // 2), (GROUP // 2, GROUP)]
@@ -100,11 +105,11 @@ def tile_nntransformlearner_pb_t_kernel(tc, G, x_next, out):
                 p_tiles[q] = ppool.tile([P, GROUP, K], BF16, name="p_sb")
             if sum_on_scalar(n):
                 return
-            nc.vector.scalar_tensor_tensor(
+            nc.vector.tensor_scalar(
                 out=junk[:, j, :],
-                in0=g_tiles[q][:, j, 0 : K // 2],
-                scalar=1.0,
-                in1=g_tiles[q][:, j, K // 2 : K],
+                in0=g_tiles[q][:, j, :],
+                scalar1=1.0,
+                scalar2=None,
                 op0=MULT,
                 op1=ADD,
                 accum_out=sums_t[q][:, j, 0:1],
@@ -115,6 +120,16 @@ def tile_nntransformlearner_pb_t_kernel(tc, G, x_next, out):
 
         def normalise(n):
             q, j = divmod(n, GROUP)
+            if norm_on_gpsimd(n):
+                nc.gpsimd.tensor_scalar(
+                    out=p_tiles[q][:, j, :],
+                    in0=g_tiles[q][:, j, :],
+                    scalar1=recip_t[q][:, j : j + 1],
+                    scalar2=0.0,
+                    op0=MULT,
+                    op1=ADD,
+                )
+                return
             nc.vector.tensor_scalar(
                 out=p_tiles[q][:, j, :],
                 in0=g_tiles[q][:, j, :],
@@ -175,7 +190,7 @@ def tile_nntransformlearner_pb_t_kernel(tc, G, x_next, out):
                 nc.sync.dma_start(out=x_raw[:], in_=x_next.rearrange("(p t) d -> p t d", t=PACK))
         ident = const.tile([P, P], F32)
         make_identity(nc, ident[:])
-        junk = const.tile([P, GROUP, K // 2], F32)
+        junk = const.tile([P, GROUP, K], BF16)
         junk_s = const.tile([P, 2, K], BF16)
         x_grouped = const.tile([P, D, PACK], BF16, align_bytes=64)
         x_codes = const.tile([P, D], U32, align_bytes=64)
@@ -200,9 +215,8 @@ def tile_nntransformlearner_pb_t_kernel(tc, G, x_next, out):
                     row_sum(j + 1)
                     reciprocals(0, j, j + 1)
                     normalise(j)
-            elif s < QUADS:
                 for j in range(1, GROUP):
-                    row_sum(s * GROUP + j)
+                    row_sum(GROUP + j)
             if 0 <= s - LAG < QUADS:
                 for first, last in pieces(s - LAG):
                     quantise(s - LAG, first, last)
@@ -215,10 +229,15 @@ def tile_nntransformlearner_pb_t_kernel(tc, G, x_next, out):
                 store(s - LAG - 1, first, last, nc.vector.tensor_copy)
             if 0 < s < QUADS:
                 reciprocals(s, 0, GROUP)
-                if s + 1 < QUADS:
-                    row_sum((s + 1) * GROUP)
                 for j in range(GROUP):
-                    normalise(s * GROUP + j)
+                    if norm_on_gpsimd(s * GROUP + j):
+                        normalise(s * GROUP + j)
+                if s + 1 < QUADS:
+                    for j in range(GROUP):
+                        row_sum((s + 1) * GROUP + j)
+                for j in range(GROUP):
+                    if not norm_on_gpsimd(s * GROUP + j):
+                        normalise(s * GROUP + j)
             if s == 2:
                 nc.vector.quantize_mx(
                     out=x_codes[:].bitcast(FP8X4),

@@ -16,6 +16,7 @@ M, K, D = 16384, 512, 128
 PACK = 4
 TILES = M // P
 GROUP = 4
+PER_BANK = 2
 QUADS = TILES // GROUP
 FLOPS = 2 * M * K * D
 
@@ -61,8 +62,8 @@ def tile_nntransformlearner_pb_t_kernel(tc, G, x_next, out):
                 return True
             return E_ON_V_EVERY > 0 and q % E_ON_V_EVERY == E_ON_V_EVERY - 1
 
-        def c_on_vector(n):
-            return n >= TILES - GROUP * TAIL_C and n % 2 == 1
+        def c_on_vector(q, first):
+            return q >= QUADS - TAIL_C and first % 2 == 1
 
         def sum_on_scalar(n):
             q, j = divmod(n, GROUP)
@@ -138,19 +139,25 @@ def tile_nntransformlearner_pb_t_kernel(tc, G, x_next, out):
                 op0=MULT,
             )
 
-        def transpose(n):
-            q, j = divmod(n, GROUP)
-            xt = psum_t.tile([P, 2, P], F32, name="xt")
-            xt_t[n] = xt
-            words = p_tiles[q][:, j, :].bitcast(F32)
-            for u in range(2):
-                nc.tensor.transpose(xt[:, u, :], words[:, u : K // 2 : 2], ident[:])
+        def runs(q):
+            size = 1 if q == QUADS - 1 else PER_BANK
+            return [(j, j + size) for j in range(0, GROUP, size)]
 
-        def regroup(n, engine_copy):
-            q, j = divmod(n, GROUP)
+        def transpose(q, first, last):
+            xt = psum_t.tile([P, PER_BANK, 2, P], F32, name="xt")
+            xt_t[q, first] = xt
+            for j in range(first, last):
+                words = p_tiles[q][:, j, :].bitcast(F32)
+                for u in range(2):
+                    nc.tensor.transpose(xt[:, j - first, u, :], words[:, u : K // 2 : 2], ident[:])
+
+        def regroup(q, first, last, engine_copy):
             engine_copy(
-                out=grouped_t[q][:, j, :, :].rearrange("p m t -> p (m t)").bitcast(F32).rearrange("p (m u) -> p m u", u=2),
-                in_=xt_t[n][:].rearrange("p u m -> p m u"),
+                out=grouped_t[q][:, first:last, :, :]
+                .rearrange("p j m t -> p (j m t)")
+                .bitcast(F32)
+                .rearrange("p (j m u) -> p j m u", j=last - first, u=2),
+                in_=xt_t[q, first][:, 0 : last - first, :, :].rearrange("p j u m -> p j m u"),
             )
 
         def quantise(q, first, last):
@@ -221,9 +228,9 @@ def tile_nntransformlearner_pb_t_kernel(tc, G, x_next, out):
                 for first, last in pieces(s - LAG):
                     quantise(s - LAG, first, last)
             if 0 <= s - 1 < QUADS:
-                for j in range(GROUP):
-                    if c_on_vector((s - 1) * GROUP + j):
-                        regroup((s - 1) * GROUP + j, nc.vector.tensor_copy)
+                for first, last in runs(s - 1):
+                    if c_on_vector(s - 1, first):
+                        regroup(s - 1, first, last, nc.vector.tensor_copy)
             if 0 <= s - LAG - 1 < QUADS and e_on_vector(s - LAG - 1):
                 first, last = pieces(s - LAG - 1)[-1]
                 store(s - LAG - 1, first, last, nc.vector.tensor_copy)
@@ -251,10 +258,10 @@ def tile_nntransformlearner_pb_t_kernel(tc, G, x_next, out):
                         store(s - LAG, first, last, nc.scalar.copy)
             if s < QUADS:
                 grouped_t[s] = qpool.tile([P, GROUP, P, PACK], BF16, name="grouped", align_bytes=64)
-                for j in range(GROUP):
-                    transpose(s * GROUP + j)
-                for j in range(GROUP):
-                    if not c_on_vector(s * GROUP + j):
-                        regroup(s * GROUP + j, nc.scalar.copy)
+                for first, last in runs(s):
+                    transpose(s, first, last)
+                for first, last in runs(s):
+                    if not c_on_vector(s, first):
+                        regroup(s, first, last, nc.scalar.copy)
             if s == 0:
                 nc.scalar.copy(out=x_grouped[:], in_=x_raw[:].rearrange("p t d -> p d t"))

@@ -42,7 +42,7 @@ def tile_nntransformlearner_pb_t_kernel(tc, G, x_next, out):
         ppool = ctx.enter_context(tc.tile_pool(name="ppool", bufs=3))
         qpool = ctx.enter_context(tc.tile_pool(name="qpool", bufs=LAG + 2))
         cpool = ctx.enter_context(tc.tile_pool(name="cpool", bufs=3))
-        opool = ctx.enter_context(tc.tile_pool(name="opool", bufs=4))
+        opool = ctx.enter_context(tc.tile_pool(name="opool", bufs=8))
         psum_t = ctx.enter_context(tc.psum_pool(name="psum_t", bufs=5))
         psum_o = ctx.enter_context(tc.psum_pool(name="psum_o", bufs=3))
         ctx.enter_context(tc.manual_schedule())
@@ -67,7 +67,7 @@ def tile_nntransformlearner_pb_t_kernel(tc, G, x_next, out):
 
         def sum_on_scalar(n):
             q, j = divmod(n, GROUP)
-            return j == S_SUM_TILE and 0 < q < QUADS
+            return j == S_SUM_TILE or (q == 0 and j % 2 == 1)
 
         def norm_on_gpsimd(n):
             q, j = divmod(n, GROUP)
@@ -208,7 +208,6 @@ def tile_nntransformlearner_pb_t_kernel(tc, G, x_next, out):
             for j in range(GROUP):
                 if sum_on_scalar(q * GROUP + j):
                     row_sum_scalar(q * GROUP + j)
-        row_sum(0)
         for s in range(QUADS + LAG + 2):
             if s + AHEAD < QUADS:
                 load(s + AHEAD)
@@ -218,11 +217,14 @@ def tile_nntransformlearner_pb_t_kernel(tc, G, x_next, out):
                     if sum_on_scalar((s + S_SUM_AHEAD) * GROUP + j):
                         row_sum_scalar((s + S_SUM_AHEAD) * GROUP + j)
             if s == 0:
-                for j in range(GROUP):
+                for j in range(0, GROUP, 2):
+                    row_sum(j)
                     row_sum(j + 1)
+                for j in range(GROUP):
                     reciprocals(0, j, j + 1)
+                for j in range(GROUP):
                     normalise(j)
-                for j in range(1, GROUP):
+                for j in range(GROUP):
                     row_sum(GROUP + j)
             if 0 <= s - LAG < QUADS:
                 for first, last in pieces(s - LAG):

@@ -69,6 +69,9 @@ def tile_nntransformlearner_pb_t_kernel(tc, G, x_next, out):
             q, j = divmod(n, GROUP)
             return j == S_SUM_TILE or (q == 0 and j % 2 == 1)
 
+        def words_apart(row):
+            return row.rearrange("p (k u e) -> p u k e", u=2, e=2)
+
         def norm_on_gpsimd(n):
             q, j = divmod(n, GROUP)
             return j == G_NORM_TILE and 0 < q < QUADS - 1
@@ -103,7 +106,7 @@ def tile_nntransformlearner_pb_t_kernel(tc, G, x_next, out):
         def row_sum(n):
             q, j = divmod(n, GROUP)
             if j == 0:
-                p_tiles[q] = ppool.tile([P, GROUP, K], BF16, name="p_sb")
+                p_tiles[q] = ppool.tile([P, GROUP, 2, P, 2], BF16, name="p_sb")
             if sum_on_scalar(n):
                 return
             nc.vector.tensor_scalar(
@@ -123,8 +126,8 @@ def tile_nntransformlearner_pb_t_kernel(tc, G, x_next, out):
             q, j = divmod(n, GROUP)
             if norm_on_gpsimd(n):
                 nc.gpsimd.tensor_scalar(
-                    out=p_tiles[q][:, j, :],
-                    in0=g_tiles[q][:, j, :],
+                    out=p_tiles[q][:, j, :, :, :],
+                    in0=words_apart(g_tiles[q][:, j, :]),
                     scalar1=recip_t[q][:, j : j + 1],
                     scalar2=0.0,
                     op0=MULT,
@@ -132,8 +135,8 @@ def tile_nntransformlearner_pb_t_kernel(tc, G, x_next, out):
                 )
                 return
             nc.vector.tensor_scalar(
-                out=p_tiles[q][:, j, :],
-                in0=g_tiles[q][:, j, :],
+                out=p_tiles[q][:, j, :, :, :],
+                in0=words_apart(g_tiles[q][:, j, :]),
                 scalar1=recip_t[q][:, j : j + 1],
                 scalar2=None,
                 op0=MULT,
@@ -147,9 +150,9 @@ def tile_nntransformlearner_pb_t_kernel(tc, G, x_next, out):
             xt = psum_t.tile([P, PER_BANK, 2, P], F32, name="xt")
             xt_t[q, first] = xt
             for j in range(first, last):
-                words = p_tiles[q][:, j, :].bitcast(F32)
                 for u in range(2):
-                    nc.tensor.transpose(xt[:, j - first, u, :], words[:, u : K // 2 : 2], ident[:])
+                    words = p_tiles[q][:, j, u, :, :].rearrange("p k e -> p (k e)").bitcast(F32)
+                    nc.tensor.transpose(xt[:, j - first, u, :], words, ident[:])
 
         def regroup(q, first, last, engine_copy):
             engine_copy(

@@ -26,6 +26,7 @@ TAIL_C = 1
 TAIL_E = 1
 E_ON_V_EVERY = 0
 S_SUM_TILE = 1
+T_SUM_TILE = 2
 G_NORM_TILE = 0
 S_SUM_AHEAD = 2
 COPY = mybir.ActivationFunctionType.Copy
@@ -44,7 +45,8 @@ def tile_nntransformlearner_pb_t_kernel(tc, G, x_next, out):
         cpool = ctx.enter_context(tc.tile_pool(name="cpool", bufs=3))
         opool = ctx.enter_context(tc.tile_pool(name="opool", bufs=8))
         psum_t = ctx.enter_context(tc.psum_pool(name="psum_t", bufs=5))
-        psum_o = ctx.enter_context(tc.psum_pool(name="psum_o", bufs=3))
+        psum_o = ctx.enter_context(tc.psum_pool(name="psum_o", bufs=2))
+        psum_s = ctx.enter_context(tc.psum_pool(name="psum_s", bufs=1))
         ctx.enter_context(tc.manual_schedule())
 
         g_tiles = {}
@@ -56,6 +58,7 @@ def tile_nntransformlearner_pb_t_kernel(tc, G, x_next, out):
         codes_t = {}
         scales_t = {}
         acc_t = {}
+        folded_t = {}
 
         def e_on_vector(q):
             if q >= QUADS - TAIL_E:
@@ -67,7 +70,41 @@ def tile_nntransformlearner_pb_t_kernel(tc, G, x_next, out):
 
         def sum_on_scalar(n):
             q, j = divmod(n, GROUP)
-            return j == S_SUM_TILE or (q == 0 and j % 2 == 1)
+            if q == 0:
+                return j % 2 == 1
+            return j == S_SUM_TILE and not sum_on_tensor(q * GROUP + T_SUM_TILE)
+
+        def sum_on_tensor(n):
+            q, j = divmod(n, GROUP)
+            return j == T_SUM_TILE and q % 5 in (0, 3) and 0 < q < QUADS - 1
+
+        def fold(n):
+            q, j = divmod(n, GROUP)
+            folded_t[n] = psum_s.tile([P, P], F32, name="folded")
+            for c in range(K // P):
+                nc.tensor.matmul(
+                    out=folded_t[n][:],
+                    lhsT=ident_b[:],
+                    rhs=g_tiles[q][:, j, c * P : (c + 1) * P],
+                    start=c == 0,
+                    stop=c == K // P - 1,
+                )
+
+        def row_sum_folded(n):
+            q, j = divmod(n, GROUP)
+            nc.scalar.activation(
+                out=junk_f[:],
+                in_=folded_t[n][:],
+                func=COPY,
+                accum_out=sums_t[q][:, j, 0:1],
+            )
+
+        def scalar_sums(q):
+            for j in range(GROUP):
+                if sum_on_scalar(q * GROUP + j):
+                    row_sum_scalar(q * GROUP + j)
+                elif sum_on_tensor(q * GROUP + j):
+                    row_sum_folded(q * GROUP + j)
 
         def words_apart(row):
             return row.rearrange("p (k u e) -> p u k e", u=2, e=2)
@@ -107,7 +144,7 @@ def tile_nntransformlearner_pb_t_kernel(tc, G, x_next, out):
             q, j = divmod(n, GROUP)
             if j == 0:
                 p_tiles[q] = ppool.tile([P, GROUP, 2, P, 2], BF16, name="p_sb")
-            if sum_on_scalar(n):
+            if sum_on_scalar(n) or sum_on_tensor(n):
                 return
             nc.vector.tensor_scalar(
                 out=junk[:, j, :],
@@ -200,6 +237,9 @@ def tile_nntransformlearner_pb_t_kernel(tc, G, x_next, out):
                 nc.sync.dma_start(out=x_raw[:], in_=x_next.rearrange("(p t) d -> p t d", t=PACK))
         ident = const.tile([P, P], F32)
         make_identity(nc, ident[:])
+        ident_b = const.tile([P, P], BF16)
+        make_identity(nc, ident_b[:])
+        junk_f = const.tile([P, P], BF16)
         junk = const.tile([P, GROUP, K], BF16)
         junk_s = const.tile([P, 2, K], BF16)
         x_grouped = const.tile([P, D, PACK], BF16, align_bytes=64)
@@ -208,17 +248,13 @@ def tile_nntransformlearner_pb_t_kernel(tc, G, x_next, out):
 
         for q in range(S_SUM_AHEAD):
             new_quad(q)
-            for j in range(GROUP):
-                if sum_on_scalar(q * GROUP + j):
-                    row_sum_scalar(q * GROUP + j)
+            scalar_sums(q)
         for s in range(QUADS + LAG + 2):
             if s + AHEAD < QUADS:
                 load(s + AHEAD)
             if s + S_SUM_AHEAD < QUADS:
                 new_quad(s + S_SUM_AHEAD)
-                for j in range(GROUP):
-                    if sum_on_scalar((s + S_SUM_AHEAD) * GROUP + j):
-                        row_sum_scalar((s + S_SUM_AHEAD) * GROUP + j)
+                scalar_sums(s + S_SUM_AHEAD)
             if s == 0:
                 for j in range(0, GROUP, 2):
                     row_sum(j)
@@ -265,6 +301,9 @@ def tile_nntransformlearner_pb_t_kernel(tc, G, x_next, out):
                 grouped_t[s] = qpool.tile([P, GROUP, P, PACK], BF16, name="grouped", align_bytes=64)
                 for first, last in runs(s):
                     transpose(s, first, last)
+                for j in range(GROUP):
+                    if s + 3 < QUADS and sum_on_tensor((s + 3) * GROUP + j):
+                        fold((s + 3) * GROUP + j)
                 for first, last in runs(s):
                     if not c_on_vector(s, first):
                         regroup(s, first, last, nc.scalar.copy)

@@ -22,9 +22,6 @@ FLOPS = 2 * M * K * D
 
 LAG = 4
 AHEAD = 8
-TAIL_C = 1
-TAIL_E = 1
-E_ON_V_EVERY = 0
 S_SUM_TILE = 1
 T_SUM_TILE = 2
 G_NORM_TILE = 0
@@ -60,19 +57,11 @@ def tile_nntransformlearner_pb_t_kernel(tc, G, x_next, out):
         acc_t = {}
         folded_t = {}
 
-        def e_on_vector(q):
-            if q >= QUADS - TAIL_E:
-                return True
-            return E_ON_V_EVERY > 0 and q % E_ON_V_EVERY == E_ON_V_EVERY - 1
-
-        def c_on_vector(q, first):
-            return q >= QUADS - TAIL_C and first % 2 == 1
-
         def sum_on_scalar(n):
             q, j = divmod(n, GROUP)
             if q == 0:
                 return j % 2 == 1
-            return j == S_SUM_TILE and not sum_on_tensor(q * GROUP + T_SUM_TILE)
+            return j == S_SUM_TILE
 
         def sum_on_tensor(n):
             q, j = divmod(n, GROUP)
@@ -180,8 +169,7 @@ def tile_nntransformlearner_pb_t_kernel(tc, G, x_next, out):
             )
 
         def runs(q):
-            size = 1 if q == QUADS - 1 else PER_BANK
-            return [(j, j + size) for j in range(0, GROUP, size)]
+            return [(j, j + PER_BANK) for j in range(0, GROUP, PER_BANK)]
 
         def transpose(q, first, last):
             xt = psum_t.tile([P, PER_BANK, 2, P], F32, name="xt")
@@ -191,8 +179,8 @@ def tile_nntransformlearner_pb_t_kernel(tc, G, x_next, out):
                     words = p_tiles[q][:, j, u, :, :].rearrange("p k e -> p (k e)").bitcast(F32)
                     nc.tensor.transpose(xt[:, j - first, u, :], words, ident[:])
 
-        def regroup(q, first, last, engine_copy):
-            engine_copy(
+        def regroup(q, first, last):
+            nc.scalar.copy(
                 out=grouped_t[q][:, first:last, :, :]
                 .rearrange("p j m t -> p (j m t)")
                 .bitcast(F32)
@@ -223,9 +211,9 @@ def tile_nntransformlearner_pb_t_kernel(tc, G, x_next, out):
                     stop=True,
                 )
 
-        def store(q, first, last, engine_copy):
+        def store(q, first, last):
             o_sb = opool.tile([P, GROUP, D], F32, name="o_sb")
-            engine_copy(out=o_sb[:, first:last, :], in_=acc_t[q, first][:, first:last, :])
+            nc.scalar.copy(out=o_sb[:, first:last, :], in_=acc_t[q, first][:, first:last, :])
             nc.sync.dma_start(
                 out=out_view[:, q * GROUP + first : q * GROUP + last, :], in_=o_sb[:, first:last, :]
             )
@@ -268,13 +256,6 @@ def tile_nntransformlearner_pb_t_kernel(tc, G, x_next, out):
             if 0 <= s - LAG < QUADS:
                 for first, last in pieces(s - LAG):
                     quantise(s - LAG, first, last)
-            if 0 <= s - 1 < QUADS:
-                for first, last in runs(s - 1):
-                    if c_on_vector(s - 1, first):
-                        regroup(s - 1, first, last, nc.vector.tensor_copy)
-            if 0 <= s - LAG - 1 < QUADS and e_on_vector(s - LAG - 1):
-                first, last = pieces(s - LAG - 1)[-1]
-                store(s - LAG - 1, first, last, nc.vector.tensor_copy)
             if 0 < s < QUADS:
                 reciprocals(s, 0, GROUP)
                 for j in range(GROUP):
@@ -295,8 +276,7 @@ def tile_nntransformlearner_pb_t_kernel(tc, G, x_next, out):
             if 0 <= s - LAG < QUADS:
                 for first, last in pieces(s - LAG):
                     multiply(s - LAG, first, last)
-                    if last < GROUP or not e_on_vector(s - LAG):
-                        store(s - LAG, first, last, nc.scalar.copy)
+                    store(s - LAG, first, last)
             if s < QUADS:
                 grouped_t[s] = qpool.tile([P, GROUP, P, PACK], BF16, name="grouped", align_bytes=64)
                 for first, last in runs(s):
@@ -305,7 +285,6 @@ def tile_nntransformlearner_pb_t_kernel(tc, G, x_next, out):
                     if s + 3 < QUADS and sum_on_tensor((s + 3) * GROUP + j):
                         fold((s + 3) * GROUP + j)
                 for first, last in runs(s):
-                    if not c_on_vector(s, first):
-                        regroup(s, first, last, nc.scalar.copy)
+                    regroup(s, first, last)
             if s == 0:
                 nc.scalar.copy(out=x_grouped[:], in_=x_raw[:].rearrange("p t d -> p d t"))

from contextlib import ExitStack

import concourse.mybir as mybir
from concourse.masks import make_identity

F32 = mybir.dt.float32
BF16 = mybir.dt.bfloat16
U32 = mybir.dt.uint32
U8 = mybir.dt.uint8
FP8X4 = mybir.dt.float8_e4m3fn_x4
MULT = mybir.AluOpType.mult
ADD = mybir.AluOpType.add

P = 128
M, K, D = 16384, 512, 128
PACK = 4
TILES = M // P
GROUP = 4
PER_BANK = 2
QUADS = TILES // GROUP
FLOPS = 2 * M * K * D

LAG = 4
AHEAD = 8
S_SUM_TILE = 1
T_SUM_TILE = 2
G_NORM_TILE = 0
S_SUM_AHEAD = 2
COPY = mybir.ActivationFunctionType.Copy


def tile_nntransformlearner_pb_t_kernel(tc, G, x_next, out):
    nc = tc.nc
    g_view = G.rearrange("(p c) k -> p c k", c=TILES)
    out_view = out.rearrange("(p c) d -> p c d", c=TILES)
    with ExitStack() as ctx:
        const = ctx.enter_context(tc.tile_pool(name="const", bufs=1))
        gpool = ctx.enter_context(tc.tile_pool(name="gpool", bufs=AHEAD + 2))
        small = ctx.enter_context(tc.tile_pool(name="small", bufs=6))
        ppool = ctx.enter_context(tc.tile_pool(name="ppool", bufs=3))
        qpool = ctx.enter_context(tc.tile_pool(name="qpool", bufs=LAG + 2))
        cpool = ctx.enter_context(tc.tile_pool(name="cpool", bufs=3))
        opool = ctx.enter_context(tc.tile_pool(name="opool", bufs=8))
        psum_t = ctx.enter_context(tc.psum_pool(name="psum_t", bufs=5))
        psum_o = ctx.enter_context(tc.psum_pool(name="psum_o", bufs=2))
        psum_s = ctx.enter_context(tc.psum_pool(name="psum_s", bufs=1))
        ctx.enter_context(tc.manual_schedule())

        g_tiles = {}
        sums_t = {}
        recip_t = {}
        p_tiles = {}
        xt_t = {}
        grouped_t = {}
        codes_t = {}
        scales_t = {}
        acc_t = {}
        folded_t = {}

        def sum_on_scalar(n):
            q, j = divmod(n, GROUP)
            if q == 0:
                return j % 2 == 1
            return j == S_SUM_TILE

        def sum_on_tensor(n):
            q, j = divmod(n, GROUP)
            return j == T_SUM_TILE and q % 5 in (0, 3) and 0 < q < QUADS - 1

        def fold(n):
            q, j = divmod(n, GROUP)
            folded_t[n] = psum_s.tile([P, P], F32, name="folded")
            for c in range(K // P):
                nc.tensor.matmul(
                    out=folded_t[n][:],
                    lhsT=ident_b[:],
                    rhs=g_tiles[q][:, j, c * P : (c + 1) * P],
                    start=c == 0,
                    stop=c == K // P - 1,
                )

        def row_sum_folded(n):
            q, j = divmod(n, GROUP)
            nc.scalar.activation(
                out=junk_f[:],
                in_=folded_t[n][:],
                func=COPY,
                accum_out=sums_t[q][:, j, 0:1],
            )

        def scalar_sums(q):
            for j in range(GROUP):
                if sum_on_scalar(q * GROUP + j):
                    row_sum_scalar(q * GROUP + j)
                elif sum_on_tensor(q * GROUP + j):
                    row_sum_folded(q * GROUP + j)

        def words_apart(row):
            return row.rearrange("p (k u e) -> p u k e", u=2, e=2)

        def norm_on_gpsimd(n):
            q, j = divmod(n, GROUP)
            return j == G_NORM_TILE and 0 < q < QUADS - 1

        def pieces(q):
            if q == QUADS - 1:
                return [(0, GROUP // 2), (GROUP // 2, GROUP)]
            return [(0, GROUP)]

        def load(q):
            g_sb = gpool.tile([P, GROUP, K], BF16, name="g_sb")
            g_tiles[q] = g_sb
            if q == 0:
                for j in range(GROUP):
                    nc.sync.dma_start(out=g_sb[:, j, :], in_=g_view[:, j, :])
            else:
                nc.sync.dma_start(out=g_sb[:], in_=g_view[:, q * GROUP : (q + 1) * GROUP, :])

        def new_quad(q):
            sums_t[q] = small.tile([P, GROUP, 8], F32, name="sums")
            recip_t[q] = small.tile([P, GROUP], F32, name="recip")

        def row_sum_scalar(n):
            q, j = divmod(n, GROUP)
            nc.scalar.activation(
                out=junk_s[:, q % 2, :],
                in_=g_tiles[q][:, j, :],
                func=COPY,
                accum_out=sums_t[q][:, j, 0:1],
            )

        def row_sum(n):
            q, j = divmod(n, GROUP)
            if j == 0:
                p_tiles[q] = ppool.tile([P, GROUP, 2, P, 2], BF16, name="p_sb")
            if sum_on_scalar(n) or sum_on_tensor(n):
                return
            nc.vector.tensor_scalar(
                out=junk[:, j, :],
                in0=g_tiles[q][:, j, :],
                scalar1=1.0,
                scalar2=None,
                op0=MULT,
                op1=ADD,
                accum_out=sums_t[q][:, j, 0:1],
            )

        def reciprocals(q, first, last):
            nc.vector.reciprocal(recip_t[q][:, first:last], sums_t[q][:, first:last, 0])

        def normalise(n):
            q, j = divmod(n, GROUP)
            if norm_on_gpsimd(n):
                nc.gpsimd.tensor_scalar(
                    out=p_tiles[q][:, j, :, :, :],
                    in0=words_apart(g_tiles[q][:, j, :]),
                    scalar1=recip_t[q][:, j : j + 1],
                    scalar2=0.0,
                    op0=MULT,
                    op1=ADD,
                )
                return
            nc.vector.tensor_scalar(
                out=p_tiles[q][:, j, :, :, :],
                in0=words_apart(g_tiles[q][:, j, :]),
                scalar1=recip_t[q][:, j : j + 1],
                scalar2=None,
                op0=MULT,
            )

        def runs(q):
            return [(j, j + PER_BANK) for j in range(0, GROUP, PER_BANK)]

        def transpose(q, first, last):
            xt = psum_t.tile([P, PER_BANK, 2, P], F32, name="xt")
            xt_t[q, first] = xt
            for j in range(first, last):
                for u in range(2):
                    words = p_tiles[q][:, j, u, :, :].rearrange("p k e -> p (k e)").bitcast(F32)
                    nc.tensor.transpose(xt[:, j - first, u, :], words, ident[:])

        def regroup(q, first, last):
            nc.scalar.copy(
                out=grouped_t[q][:, first:last, :, :]
                .rearrange("p j m t -> p (j m t)")
                .bitcast(F32)
                .rearrange("p (j m u) -> p j m u", j=last - first, u=2),
                in_=xt_t[q, first][:, 0 : last - first, :, :].rearrange("p j u m -> p j m u"),
            )

        def quantise(q, first, last):
            if first == 0:
                codes_t[q] = cpool.tile([P, GROUP * P], U32, name="codes", align_bytes=64)
                scales_t[q] = cpool.tile([P, GROUP * P], U8, name="scales", align_bytes=64)
            nc.vector.quantize_mx(
                out=codes_t[q][:, first * P : last * P].bitcast(FP8X4),
                scales=scales_t[q][:, first * P : last * P],
                in_=grouped_t[q][:, first:last, :, :].rearrange("p j m t -> p (j m t)"),
            )

        def multiply(q, first, last):
            acc_t[q, first] = psum_o.tile([P, GROUP, D], F32, name="acc")
            for j in range(first, last):
                nc.tensor.matmul_mx(
                    out=acc_t[q, first][:, j, :],
                    lhsT=codes_t[q][:, j * P : (j + 1) * P].bitcast(FP8X4),
                    lhsT_scale=scales_t[q][:, j * P : (j + 1) * P],
                    rhs=x_codes[:].bitcast(FP8X4),
                    rhs_scale=x_scales[:],
                    start=True,
                    stop=True,
                )

        def store(q, first, last):
            o_sb = opool.tile([P, GROUP, D], F32, name="o_sb")
            nc.scalar.copy(out=o_sb[:, first:last, :], in_=acc_t[q, first][:, first:last, :])
            nc.sync.dma_start(
                out=out_view[:, q * GROUP + first : q * GROUP + last, :], in_=o_sb[:, first:last, :]
            )

        x_raw = const.tile([P, PACK, D], BF16)
        for q in range(AHEAD):
            load(q)
            if q == 1:
                nc.sync.dma_start(out=x_raw[:], in_=x_next.rearrange("(p t) d -> p t d", t=PACK))
        ident = const.tile([P, P], F32)
        make_identity(nc, ident[:])
        ident_b = const.tile([P, P], BF16)
        make_identity(nc, ident_b[:])
        junk_f = const.tile([P, P], BF16)
        junk = const.tile([P, GROUP, K], BF16)
        junk_s = const.tile([P, 2, K], BF16)
        x_grouped = const.tile([P, D, PACK], BF16, align_bytes=64)
        x_codes = const.tile([P, D], U32, align_bytes=64)
        x_scales = const.tile([P, D], U8, align_bytes=64)

        for q in range(S_SUM_AHEAD):
            new_quad(q)
            scalar_sums(q)
        for s in range(QUADS + LAG + 2):
            if s + AHEAD < QUADS:
                load(s + AHEAD)
            if s + S_SUM_AHEAD < QUADS:
                new_quad(s + S_SUM_AHEAD)
                scalar_sums(s + S_SUM_AHEAD)
            if s == 0:
                for j in range(0, GROUP, 2):
                    row_sum(j)
                    row_sum(j + 1)
                for j in range(GROUP):
                    reciprocals(0, j, j + 1)
                for j in range(GROUP):
                    normalise(j)
                for j in range(GROUP):
                    row_sum(GROUP + j)
            if 0 <= s - LAG < QUADS:
                for first, last in pieces(s - LAG):
                    quantise(s - LAG, first, last)
            if 0 < s < QUADS:
                reciprocals(s, 0, GROUP)
                for j in range(GROUP):
                    if norm_on_gpsimd(s * GROUP + j):
                        normalise(s * GROUP + j)
                if s + 1 < QUADS:
                    for j in range(GROUP):
                        row_sum((s + 1) * GROUP + j)
                for j in range(GROUP):
                    if not norm_on_gpsimd(s * GROUP + j):
                        normalise(s * GROUP + j)
            if s == 2:
                nc.vector.quantize_mx(
                    out=x_codes[:].bitcast(FP8X4),
                    scales=x_scales[:],
                    in_=x_grouped[:].rearrange("p d t -> p (d t)"),
                )
            if 0 <= s - LAG < QUADS:
                for first, last in pieces(s - LAG):
                    multiply(s - LAG, first, last)
                    store(s - LAG, first, last)
            if s < QUADS:
                grouped_t[s] = qpool.tile([P, GROUP, P, PACK], BF16, name="grouped", align_bytes=64)
                for first, last in runs(s):
                    transpose(s, first, last)
                for j in range(GROUP):
                    if s + 3 < QUADS and sum_on_tensor((s + 3) * GROUP + j):
                        fold((s + 3) * GROUP + j)
                for first, last in runs(s):
                    regroup(s, first, last)
            if s == 0:
                nc.scalar.copy(out=x_grouped[:], in_=x_raw[:].rearrange("p t d -> p d t"))
